import numpy as np
import ml_dtypes


def mxq(x, axis, fmt="e4m3"):
    dtype, down = {"e4m3": (ml_dtypes.float8_e4m3fn, 7), "e5m2": (ml_dtypes.float8_e5m2, 14)}[fmt]
    v = np.moveaxis(np.asarray(x, np.float32).astype(ml_dtypes.bfloat16).astype(np.float64), axis, -1)
    blocks = v.reshape(v.shape[:-1] + (-1, 32))
    amax = np.abs(blocks).max(-1, keepdims=True)
    byte = np.maximum(np.where(amax > 0, np.frexp(amax)[1] - 1 + 127, 0) - down, 1)
    scale = np.exp2(byte - 127.0)
    codes = (blocks / scale).astype(np.float32).astype(dtype).astype(np.float64)
    return np.moveaxis((codes * scale).reshape(v.shape), -1, axis)


WIDE = False


def mx_kscale(k):
    if not WIDE:
        return np.ones(k)
    levels = np.array([10, -10, 5, -5, 0])
    a = np.random.permutation(np.resize(levels, k // 512 * 4)).reshape(k // 512, 4)
    idx = np.arange(k)
    return np.exp2(a[idx // 512, idx % 128 // 32])


BF16 = ml_dtypes.bfloat16


def bf(x):
    return np.asarray(x, np.float32).astype(BF16)


def f64(x):
    return np.asarray(x).astype(np.float64)


B, S, HID, NH, DH = 4, 256, 1024, 16, 64
DQ = NH * DH


def setup_inputs():
    s = mx_kscale(HID)

    def w():
        return bf(np.random.standard_normal((HID, DQ)) / np.sqrt(HID) / s[:, None])

    def b():
        return bf(np.random.standard_normal(DQ) * 0.3)

    return {"x": bf(np.random.standard_normal((B, S, HID)) * s),
            "reasoning_mask": bf(np.random.uniform(size=(B, S, 1, 1))),
            "Wq": w(), "bq": b(), "Wk": w(), "bk": b(),
            "Wqr": w(), "bqr": b(), "Wkr": w(), "bkr": b()}


def reference(x, reasoning_mask, Wq, bq, Wk, bk, Wqr, bqr, Wkr, bkr):
    xq = mxq(f64(x), 2, "e4m3")
    g = f64(reasoning_mask)

    def proj(W, b):
        return ((xq @ mxq(f64(W), 0, "e4m3")) + f64(b)).reshape(B, S, NH, DH)

    q = proj(Wq, bq)
    k = proj(Wk, bk)
    q_r = proj(Wqr, bqr)
    k_r = proj(Wkr, bkr)
    q = q * (1.0 - g) + q_r * g
    k = k * (1.0 - g) + k_r * g
    return q, k

@@ -1,0 +1,206 @@
+from contextlib import ExitStack
+
+import concourse.mybir as mybir
+from concourse.masks import make_identity
+
+F32 = mybir.dt.float32
+BF16 = mybir.dt.bfloat16
+U32 = mybir.dt.uint32
+U8 = mybir.dt.uint8
+I32 = mybir.dt.int32
+FP8X4 = mybir.dt.float8_e4m3fn_x4
+MULT = mybir.AluOpType.mult
+ADD = mybir.AluOpType.add
+
+P = 128
+PACK = 4
+K_PASS = P * PACK
+TOKENS = 1024
+HID = 1024
+DQ = 1024
+PASSES = HID // K_PASS
+TOKEN_TILES = TOKENS // P
+N_TILE = 512
+CHUNKS = DQ // N_TILE
+RUN = 4
+REGROUP_COLS = 128
+
+FLOPS = 4 * 2 * TOKENS * HID * DQ
+
+ROW_ONE, ROW_GATE, ROW_MINUS_GATE = 0, 32, 64
+
+
+def regroup(copy, grouped, rows):
+    copy(
+        out=grouped.rearrange("p (c i) t -> p c t i", i=RUN),
+        in_=rows.rearrange("p t (c i) -> p c t i", i=RUN),
+    )
+
+
+def tile_reasoningmultiheadattention_pa_kernel(
+    tc, x, reasoning_mask, Wq, bq, Wk, bk, Wqr, bqr, Wkr, bkr, out_0, out_1
+):
+    nc = tc.nc
+    x_rows = x.flatten_outer_dims()
+    gate_row = reasoning_mask.rearrange("b s o i -> (o i) (b s)")
+    outs = [out_0.rearrange("b s h d -> (b s) (h d)"), out_1.rearrange("b s h d -> (b s) (h d)")]
+    weights = [(Wq, Wqr), (Wk, Wkr)]
+    biases = [(bq, bqr), (bk, bkr)]
+
+    with ExitStack() as stack:
+        keep = stack.enter_context(tc.tile_pool(name="keep", bufs=1))
+        stage = stack.enter_context(tc.tile_pool(name="stage", bufs=4))
+        banks = stack.enter_context(tc.psum_pool(name="banks", bufs=5))
+        side = stack.enter_context(tc.psum_pool(name="side", bufs=3))
+
+        blend_lhs = keep.tile([P, TOKENS], BF16)
+        blend_rhs = [keep.tile([P, DQ], BF16, name="blend_rhs_%d" % o) for o in range(2)]
+        ident_f32 = keep.tile([P, P], F32)
+        ident_bf16 = keep.tile([P, P], BF16)
+        x_raw = keep.tile([P, TOKEN_TILES, HID], BF16)
+        w_raw = {}
+
+        def load_bias_rows(o):
+            plain, reasoning = biases[o]
+            for row, bias in ((ROW_ONE, plain), (ROW_GATE, reasoning), (ROW_MINUS_GATE, plain)):
+                nc.sync.dma_start(
+                    out=blend_rhs[o][row : row + 1, :], in_=bias.rearrange("(o n) -> o n", o=1)
+                )
+
+        def load_weight(o, r):
+            for g in range(PASSES):
+                raw = keep.tile([P, PACK, DQ], BF16, name="w_raw_%d_%d_%d" % (o, r, g))
+                nc.sync.dma_start(
+                    out=raw[:].rearrange("q (u e) n -> q u e n", u=2),
+                    in_=weights[o][r][g * K_PASS : (g + 1) * K_PASS, :].rearrange(
+                        "(u q e) n -> q u e n", u=2, e=2
+                    ),
+                )
+                w_raw[(o, r, g)] = raw
+
+        with tc.manual_schedule():
+            nc.vector.memset(blend_lhs[:].bitcast(I32), 0)
+            nc.vector.memset(blend_lhs[ROW_ONE : ROW_ONE + 32, :], 1.0)
+            nc.vector.memset(blend_rhs[0][:].bitcast(I32), 0)
+            nc.vector.memset(blend_rhs[1][:].bitcast(I32), 0)
+            make_identity(nc, ident_bf16[:])
+            make_identity(nc, ident_f32[:])
+            nc.sync.dma_start(out=blend_lhs[ROW_GATE : ROW_GATE + 1, :], in_=gate_row)
+            nc.sync.dma_start(out=blend_lhs[ROW_MINUS_GATE : ROW_MINUS_GATE + 1, :], in_=gate_row)
+            load_bias_rows(0)
+            load_weight(0, 0)
+            for m in range(0, TOKEN_TILES, 2):
+                nc.sync.dma_start(
+                    out=x_raw[:, m : m + 2, :],
+                    in_=x_rows[m * P : (m + 2) * P, :].rearrange("(m p) k -> p m k", p=P),
+                )
+            load_bias_rows(1)
+            load_weight(0, 1)
+            load_weight(1, 0)
+            load_weight(1, 1)
+            nc.vector.tensor_scalar_mul(
+                out=blend_lhs[ROW_MINUS_GATE : ROW_MINUS_GATE + 32, :],
+                in0=blend_lhs[ROW_MINUS_GATE : ROW_MINUS_GATE + 32, :],
+                scalar1=-1.0,
+            )
+
+        lhs_t = side.tile([P, TOKEN_TILES, P], BF16, tag="side")
+        for m in range(TOKEN_TILES):
+            nc.tensor.transpose(lhs_t[:, m, :], blend_lhs[:, m * P : (m + 1) * P], ident_bf16[:])
+        gate = keep.tile([P, TOKEN_TILES], F32)
+        nc.vector.tensor_copy(out=gate[:], in_=lhs_t[:, :, ROW_GATE])
+        one_minus_gate = keep.tile([P, TOKEN_TILES], F32)
+        nc.vector.tensor_scalar(
+            out=one_minus_gate[:], in0=gate[:], scalar1=-1.0, scalar2=1.0, op0=MULT, op1=ADD
+        )
+        factor = (one_minus_gate, gate)
+
+        x_codes = keep.tile([P, TOKEN_TILES, PASSES * P], U32, align_bytes=64)
+        x_scales = keep.tile([P, TOKEN_TILES, PASSES * P], U8, align_bytes=64)
+        w_codes = keep.tile([P, 2, 2, PASSES, DQ], U32, align_bytes=64)
+        w_scales = keep.tile([P, 2, 2, PASSES, DQ], U8, align_bytes=64)
+        acc = keep.tile([P, 2, TOKEN_TILES, DQ], F32)
+
+        def blended_bias(o, c):
+            cols = slice(c * N_TILE, (c + 1) * N_TILE)
+            for m in range(TOKEN_TILES):
+                bias_bank = side.tile([P, N_TILE], F32, tag="side")
+                nc.tensor.matmul(
+                    out=bias_bank[:],
+                    lhsT=blend_lhs[:, m * P : (m + 1) * P],
+                    rhs=blend_rhs[o][:, cols],
+                    start=True,
+                    stop=True,
+                )
+                nc.any.tensor_copy(out=acc[:, o, m, cols], in_=bias_bank[:])
+
+        def quantise_weight(o, r, c):
+            cols = slice(c * N_TILE, (c + 1) * N_TILE)
+            for g in range(PASSES):
+                rows = w_raw[(o, r, g)][:, :, cols]
+                grouped = stage.tile([P, N_TILE, PACK], BF16, align_bytes=64, tag="grouped")
+                for n in range(0, N_TILE, REGROUP_COLS):
+                    regroup(
+                        nc.any.tensor_copy,
+                        grouped[:, n : n + REGROUP_COLS, :],
+                        rows[:, :, n : n + REGROUP_COLS],
+                    )
+                nc.vector.quantize_mx(
+                    out=w_codes[:, o, r, g, cols].bitcast(FP8X4),
+                    scales=w_scales[:, o, r, g, cols],
+                    in_=grouped[:].rearrange("p n t -> p (n t)"),
+                )
+
+        def quantise_tokens(m):
+            words = x_raw[:, m, :].bitcast(F32)
+            turned = side.tile([P, PASSES * 2, P], F32, tag="side")
+            for j in range(PASSES * 2):
+                nc.tensor.transpose(turned[:, j, :], words[:, j * P : (j + 1) * P], ident_f32[:])
+            x_grouped = stage.tile([P, PASSES * P * PACK], BF16, align_bytes=64, tag="x_grouped")
+            nc.any.tensor_copy(
+                out=x_grouped[:].bitcast(F32).rearrange("p (g r u) -> p g r u", g=PASSES, u=2),
+                in_=turned[:].rearrange("p (g u) r -> p g r u", u=2),
+            )
+            nc.vector.quantize_mx(
+                out=x_codes[:, m, :].bitcast(FP8X4), scales=x_scales[:, m, :], in_=x_grouped[:]
+            )
+
+        def multiply(o, r, c):
+            cols = slice(c * N_TILE, (c + 1) * N_TILE)
+            for m in range(TOKEN_TILES):
+                product = banks.tile([P, N_TILE], F32, tag="product")
+                for g in range(PASSES):
+                    tokens = slice(g * P, (g + 1) * P)
+                    nc.tensor.matmul_mx(
+                        out=product[:],
+                        lhsT=x_codes[:, m, tokens].bitcast(FP8X4),
+                        lhsT_scale=x_scales[:, m, tokens],
+                        rhs=w_codes[:, o, r, g, cols].bitcast(FP8X4),
+                        rhs_scale=w_scales[:, o, r, g, cols],
+                        start=(g == 0),
+                        stop=(g == PASSES - 1),
+                    )
+                nc.vector.scalar_tensor_tensor(
+                    out=acc[:, o, m, cols],
+                    in0=product[:],
+                    scalar=factor[r][:, m : m + 1],
+                    in1=acc[:, o, m, cols],
+                    op0=MULT,
+                    op1=ADD,
+                )
+                if r == 1:
+                    nc.sync.dma_start(out=outs[o][m * P : (m + 1) * P, cols], in_=acc[:, o, m, cols])
+
+        def prepare(o, r, c):
+            if r == 0:
+                blended_bias(o, c)
+            quantise_weight(o, r, c)
+
+        phases = [(o, r, c) for o in range(2) for r in range(2) for c in range(CHUNKS)]
+        prepare(*phases[0])
+        for m in range(TOKEN_TILES):
+            quantise_tokens(m)
+        for i, phase in enumerate(phases):
+            if i + 1 < len(phases):
+                prepare(*phases[i + 1])
+            multiply(*phase)

@@ -22,8 +22,15 @@ PASSES = HID // K_PASS
 TOKEN_TILES = TOKENS // P
 N_TILE = 512
 CHUNKS = DQ // N_TILE
+STAGES = 2 * CHUNKS
+PHASES = 2 * STAGES
+STEPS_PER_PASS = TOKEN_TILES // PASSES
+
 RUN = 4
-REGROUP_COLS = 128
+GPSIMD_COLS = 256
+SCALAR_COLS = 128
+SCALAR_COPIES = (N_TILE - GPSIMD_COLS) // SCALAR_COLS
+TOKENS_AHEAD = 2
 
 FLOPS = 4 * 2 * TOKENS * HID * DQ
 
@@ -43,22 +50,37 @@ def tile_reasoningmultiheadattention_pa_kernel(
     nc = tc.nc
     x_rows = x.flatten_outer_dims()
     gate_row = reasoning_mask.rearrange("b s o i -> (o i) (b s)")
-    outs = [out_0.rearrange("b s h d -> (b s) (h d)"), out_1.rearrange("b s h d -> (b s) (h d)")]
-    weights = [(Wq, Wqr), (Wk, Wkr)]
-    biases = [(bq, bqr), (bk, bkr)]
+    outs = (out_0.rearrange("b s h d -> (b s) (h d)"), out_1.rearrange("b s h d -> (b s) (h d)"))
+    weights = ((Wq, Wqr), (Wk, Wkr))
+    biases = ((bq, bqr), (bk, bkr))
 
     with ExitStack() as stack:
+        stack.enter_context(tc.manual_schedule())
         keep = stack.enter_context(tc.tile_pool(name="keep", bufs=1))
-        stage = stack.enter_context(tc.tile_pool(name="stage", bufs=4))
-        banks = stack.enter_context(tc.psum_pool(name="banks", bufs=5))
-        side = stack.enter_context(tc.psum_pool(name="side", bufs=3))
+        w_stage = stack.enter_context(tc.tile_pool(name="w_stage", bufs=3))
+        x_stage = stack.enter_context(tc.tile_pool(name="x_stage", bufs=4))
+        product_banks = stack.enter_context(tc.psum_pool(name="product_banks", bufs=4))
+        side_banks = stack.enter_context(tc.psum_pool(name="side_banks", bufs=4))
 
         blend_lhs = keep.tile([P, TOKENS], BF16)
         blend_rhs = [keep.tile([P, DQ], BF16, name="blend_rhs_%d" % o) for o in range(2)]
         ident_f32 = keep.tile([P, P], F32)
         ident_bf16 = keep.tile([P, P], BF16)
+        gate = keep.tile([P, TOKEN_TILES], F32)
+        one_minus_gate = keep.tile([P, TOKEN_TILES], F32)
+        factor = (one_minus_gate, gate)
         x_raw = keep.tile([P, TOKEN_TILES, HID], BF16)
-        w_raw = {}
+        w_raw = keep.tile([P, PHASES, PASSES, PACK, N_TILE], BF16)
+        x_codes = keep.tile([P, TOKEN_TILES, PASSES * P], U32, align_bytes=64)
+        x_scales = keep.tile([P, TOKEN_TILES, PASSES * P], U8, align_bytes=64)
+        w_codes = keep.tile([P, PHASES, PASSES, N_TILE], U32, align_bytes=64)
+        w_scales = keep.tile([P, PHASES, PASSES, N_TILE], U8, align_bytes=64)
+        acc = keep.tile([P, STAGES, TOKEN_TILES, N_TILE], F32)
+        grouped_of = {}
+
+        def columns(stage):
+            chunk = stage % CHUNKS
+            return slice(chunk * N_TILE, (chunk + 1) * N_TILE)
 
         def load_bias_rows(o):
             plain, reasoning = biases[o]
@@ -67,140 +89,148 @@ def tile_reasoningmultiheadattention_pa_kernel(
                     out=blend_rhs[o][row : row + 1, :], in_=bias.rearrange("(o n) -> o n", o=1)
                 )
 
-        def load_weight(o, r):
-            for g in range(PASSES):
-                raw = keep.tile([P, PACK, DQ], BF16, name="w_raw_%d_%d_%d" % (o, r, g))
-                nc.sync.dma_start(
-                    out=raw[:].rearrange("q (u e) n -> q u e n", u=2),
-                    in_=weights[o][r][g * K_PASS : (g + 1) * K_PASS, :].rearrange(
-                        "(u q e) n -> q u e n", u=2, e=2
-                    ),
-                )
-                w_raw[(o, r, g)] = raw
-
-        with tc.manual_schedule():
-            nc.vector.memset(blend_lhs[:].bitcast(I32), 0)
-            nc.vector.memset(blend_lhs[ROW_ONE : ROW_ONE + 32, :], 1.0)
-            nc.vector.memset(blend_rhs[0][:].bitcast(I32), 0)
-            nc.vector.memset(blend_rhs[1][:].bitcast(I32), 0)
-            make_identity(nc, ident_bf16[:])
-            make_identity(nc, ident_f32[:])
-            nc.sync.dma_start(out=blend_lhs[ROW_GATE : ROW_GATE + 1, :], in_=gate_row)
-            nc.sync.dma_start(out=blend_lhs[ROW_MINUS_GATE : ROW_MINUS_GATE + 1, :], in_=gate_row)
-            load_bias_rows(0)
-            load_weight(0, 0)
-            for m in range(0, TOKEN_TILES, 2):
-                nc.sync.dma_start(
-                    out=x_raw[:, m : m + 2, :],
-                    in_=x_rows[m * P : (m + 2) * P, :].rearrange("(m p) k -> p m k", p=P),
-                )
-            load_bias_rows(1)
-            load_weight(0, 1)
-            load_weight(1, 0)
-            load_weight(1, 1)
-            nc.vector.tensor_scalar_mul(
-                out=blend_lhs[ROW_MINUS_GATE : ROW_MINUS_GATE + 32, :],
-                in0=blend_lhs[ROW_MINUS_GATE : ROW_MINUS_GATE + 32, :],
-                scalar1=-1.0,
+        def load_weight(phase, g):
+            stage, r = phase // 2, phase % 2
+            nc.sync.dma_start(
+                out=w_raw[:, phase, g, :, :],
+                in_=weights[stage // CHUNKS][r][
+                    g * K_PASS : (g + 1) * K_PASS, columns(stage)
+                ].rearrange("(p t) n -> p t n", t=PACK),
             )
 
-        lhs_t = side.tile([P, TOKEN_TILES, P], BF16, tag="side")
-        for m in range(TOKEN_TILES):
-            nc.tensor.transpose(lhs_t[:, m, :], blend_lhs[:, m * P : (m + 1) * P], ident_bf16[:])
-        gate = keep.tile([P, TOKEN_TILES], F32)
-        nc.vector.tensor_copy(out=gate[:], in_=lhs_t[:, :, ROW_GATE])
-        one_minus_gate = keep.tile([P, TOKEN_TILES], F32)
-        nc.vector.tensor_scalar(
-            out=one_minus_gate[:], in0=gate[:], scalar1=-1.0, scalar2=1.0, op0=MULT, op1=ADD
-        )
-        factor = (one_minus_gate, gate)
+        def load_tokens(m):
+            nc.sync.dma_start(out=x_raw[:, m, :], in_=x_rows[m * P : (m + 1) * P, :])
 
-        x_codes = keep.tile([P, TOKEN_TILES, PASSES * P], U32, align_bytes=64)
-        x_scales = keep.tile([P, TOKEN_TILES, PASSES * P], U8, align_bytes=64)
-        w_codes = keep.tile([P, 2, 2, PASSES, DQ], U32, align_bytes=64)
-        w_scales = keep.tile([P, 2, 2, PASSES, DQ], U8, align_bytes=64)
-        acc = keep.tile([P, 2, TOKEN_TILES, DQ], F32)
+        def gpsimd_copy(out, in_):
+            nc.gpsimd.tensor_scalar(out=out, in0=in_, scalar1=1.0, scalar2=0.0, op0=MULT, op1=ADD)
 
-        def blended_bias(o, c):
-            cols = slice(c * N_TILE, (c + 1) * N_TILE)
-            for m in range(TOKEN_TILES):
-                bias_bank = side.tile([P, N_TILE], F32, tag="side")
-                nc.tensor.matmul(
-                    out=bias_bank[:],
-                    lhsT=blend_lhs[:, m * P : (m + 1) * P],
-                    rhs=blend_rhs[o][:, cols],
-                    start=True,
-                    stop=True,
+        def regroup_weight(copy, phase, g, first, count):
+            if (phase, g) not in grouped_of:
+                grouped_of[(phase, g)] = w_stage.tile(
+                    [P, N_TILE, PACK], BF16, align_bytes=64, name="grouped"
                 )
-                nc.any.tensor_copy(out=acc[:, o, m, cols], in_=bias_bank[:])
+            regroup(
+                copy,
+                grouped_of[(phase, g)][:, first : first + count, :],
+                w_raw[:, phase, g, :, first : first + count],
+            )
 
-        def quantise_weight(o, r, c):
-            cols = slice(c * N_TILE, (c + 1) * N_TILE)
-            for g in range(PASSES):
-                rows = w_raw[(o, r, g)][:, :, cols]
-                grouped = stage.tile([P, N_TILE, PACK], BF16, align_bytes=64, tag="grouped")
-                for n in range(0, N_TILE, REGROUP_COLS):
-                    regroup(
-                        nc.any.tensor_copy,
-                        grouped[:, n : n + REGROUP_COLS, :],
-                        rows[:, :, n : n + REGROUP_COLS],
-                    )
-                nc.vector.quantize_mx(
-                    out=w_codes[:, o, r, g, cols].bitcast(FP8X4),
-                    scales=w_scales[:, o, r, g, cols],
-                    in_=grouped[:].rearrange("p n t -> p (n t)"),
-                )
+        def quantise_weight(phase, g):
+            nc.vector.quantize_mx(
+                out=w_codes[:, phase, g, :].bitcast(FP8X4),
+                scales=w_scales[:, phase, g, :],
+                in_=grouped_of[(phase, g)][:].rearrange("p n t -> p (n t)"),
+            )
 
         def quantise_tokens(m):
-            words = x_raw[:, m, :].bitcast(F32)
-            turned = side.tile([P, PASSES * 2, P], F32, tag="side")
-            for j in range(PASSES * 2):
-                nc.tensor.transpose(turned[:, j, :], words[:, j * P : (j + 1) * P], ident_f32[:])
-            x_grouped = stage.tile([P, PASSES * P * PACK], BF16, align_bytes=64, tag="x_grouped")
-            nc.any.tensor_copy(
+            words = x_raw[:, m, :].bitcast(F32).rearrange("r (g p u) -> r g u p", g=PASSES, u=2)
+            turned = side_banks.tile([P, PASSES, 2, P], F32, name="side")
+            for g in range(PASSES):
+                for u in range(2):
+                    nc.tensor.transpose(turned[:, g, u, :], words[:, g, u, :], ident_f32[:])
+            x_grouped = x_stage.tile([P, PASSES * P * PACK], BF16, align_bytes=64)
+            nc.scalar.copy(
                 out=x_grouped[:].bitcast(F32).rearrange("p (g r u) -> p g r u", g=PASSES, u=2),
-                in_=turned[:].rearrange("p (g u) r -> p g r u", u=2),
+                in_=turned[:].rearrange("p g u r -> p g r u"),
             )
             nc.vector.quantize_mx(
                 out=x_codes[:, m, :].bitcast(FP8X4), scales=x_scales[:, m, :], in_=x_grouped[:]
             )
 
-        def multiply(o, r, c):
-            cols = slice(c * N_TILE, (c + 1) * N_TILE)
-            for m in range(TOKEN_TILES):
-                product = banks.tile([P, N_TILE], F32, tag="product")
-                for g in range(PASSES):
-                    tokens = slice(g * P, (g + 1) * P)
-                    nc.tensor.matmul_mx(
-                        out=product[:],
-                        lhsT=x_codes[:, m, tokens].bitcast(FP8X4),
-                        lhsT_scale=x_scales[:, m, tokens],
-                        rhs=w_codes[:, o, r, g, cols].bitcast(FP8X4),
-                        rhs_scale=w_scales[:, o, r, g, cols],
-                        start=(g == 0),
-                        stop=(g == PASSES - 1),
-                    )
-                nc.vector.scalar_tensor_tensor(
-                    out=acc[:, o, m, cols],
-                    in0=product[:],
-                    scalar=factor[r][:, m : m + 1],
-                    in1=acc[:, o, m, cols],
-                    op0=MULT,
-                    op1=ADD,
+        def blended_bias(stage, m):
+            bias_bank = side_banks.tile([P, N_TILE], F32, name="side")
+            nc.tensor.matmul(
+                out=bias_bank[:],
+                lhsT=blend_lhs[:, m * P : (m + 1) * P],
+                rhs=blend_rhs[stage // CHUNKS][:, columns(stage)],
+                start=True,
+                stop=True,
+            )
+            nc.scalar.copy(out=acc[:, stage, m, :], in_=bias_bank[:])
+
+        def multiply_and_blend(phase, m):
+            stage, r = phase // 2, phase % 2
+            product = product_banks.tile([P, N_TILE], F32)
+            for g in range(PASSES):
+                tokens = slice(g * P, (g + 1) * P)
+                nc.tensor.matmul_mx(
+                    out=product[:],
+                    lhsT=x_codes[:, m, tokens].bitcast(FP8X4),
+                    lhsT_scale=x_scales[:, m, tokens],
+                    rhs=w_codes[:, phase, g, :].bitcast(FP8X4),
+                    rhs_scale=w_scales[:, phase, g, :],
+                    start=(g == 0),
+                    stop=(g == PASSES - 1),
                 )
-                if r == 1:
-                    nc.sync.dma_start(out=outs[o][m * P : (m + 1) * P, cols], in_=acc[:, o, m, cols])
+            nc.vector.scalar_tensor_tensor(
+                out=acc[:, stage, m, :],
+                in0=product[:],
+                scalar=factor[r][:, m : m + 1],
+                in1=acc[:, stage, m, :],
+                op0=MULT,
+                op1=ADD,
+            )
+            if r == 1:
+                nc.sync.dma_start(
+                    out=outs[stage // CHUNKS][m * P : (m + 1) * P, columns(stage)],
+                    in_=acc[:, stage, m, :],
+                )
 
-        def prepare(o, r, c):
-            if r == 0:
-                blended_bias(o, c)
-            quantise_weight(o, r, c)
+        nc.vector.memset(blend_lhs[:].bitcast(I32), 0)
+        nc.vector.memset(blend_lhs[ROW_ONE : ROW_ONE + 32, :], 1.0)
+        nc.vector.memset(blend_rhs[0][:].bitcast(I32), 0)
+        nc.vector.memset(blend_rhs[1][:].bitcast(I32), 0)
+        make_identity(nc, ident_f32[:])
+        make_identity(nc, ident_bf16[:])
+        nc.sync.dma_start(out=blend_lhs[ROW_GATE : ROW_GATE + 1, :], in_=gate_row)
+        nc.sync.dma_start(out=blend_lhs[ROW_MINUS_GATE : ROW_MINUS_GATE + 1, :], in_=gate_row)
+        load_bias_rows(0)
+        for g in range(PASSES):
+            load_weight(0, g)
+        for g in range(PASSES):
+            for m in range(g * STEPS_PER_PASS, (g + 1) * STEPS_PER_PASS):
+                load_tokens(m)
+            load_weight(1, g)
+        load_bias_rows(1)
+        for phase in range(2, PHASES):
+            for g in range(PASSES):
+                load_weight(phase, g)
+        nc.vector.tensor_scalar_mul(
+            out=blend_lhs[ROW_MINUS_GATE : ROW_MINUS_GATE + 32, :],
+            in0=blend_lhs[ROW_MINUS_GATE : ROW_MINUS_GATE + 32, :],
+            scalar1=-1.0,
+        )
 
-        phases = [(o, r, c) for o in range(2) for r in range(2) for c in range(CHUNKS)]
-        prepare(*phases[0])
         for m in range(TOKEN_TILES):
+            blended_bias(0, m)
+        for g in range(PASSES):
+            regroup_weight(nc.vector.tensor_copy, 0, g, 0, N_TILE)
+            quantise_weight(0, g)
+        lhs_turned = side_banks.tile([P, TOKEN_TILES, P], BF16, name="side")
+        for m in range(TOKEN_TILES):
+            nc.tensor.transpose(lhs_turned[:, m, :], blend_lhs[:, m * P : (m + 1) * P], ident_bf16[:])
+        nc.vector.tensor_copy(out=gate[:], in_=lhs_turned[:, :, ROW_GATE])
+        nc.vector.tensor_scalar(
+            out=one_minus_gate[:], in0=gate[:], scalar1=-1.0, scalar2=1.0, op0=MULT, op1=ADD
+        )
+        for m in range(TOKENS_AHEAD):
             quantise_tokens(m)
-        for i, phase in enumerate(phases):
-            if i + 1 < len(phases):
-                prepare(*phases[i + 1])
-            multiply(*phase)
+
+        for phase in range(PHASES):
+            stage, r = phase // 2, phase % 2
+            for m in range(TOKEN_TILES):
+                g, step = m // STEPS_PER_PASS, m % STEPS_PER_PASS
+                if phase == 0 and m + TOKENS_AHEAD < TOKEN_TILES:
+                    quantise_tokens(m + TOKENS_AHEAD)
+                if phase + 1 < PHASES:
+                    if step == 0:
+                        regroup_weight(gpsimd_copy, phase + 1, g, 0, GPSIMD_COLS)
+                    if step < SCALAR_COPIES:
+                        regroup_weight(
+                            nc.scalar.copy, phase + 1, g, GPSIMD_COLS + step * SCALAR_COLS, SCALAR_COLS
+                        )
+                if stage + 1 < STAGES and m % 2 == 1:
+                    blended_bias(stage + 1, (r * TOKEN_TILES + m) // 2)
+                multiply_and_blend(phase, m)
+                if phase + 1 < PHASES and step == SCALAR_COPIES - 1:
+                    quantise_weight(phase + 1, g)

@@ -27,8 +27,8 @@ PHASES = 2 * STAGES
 STEPS_PER_PASS = TOKEN_TILES // PASSES
 
 RUN = 4
-GPSIMD_COLS = 256
-SCALAR_COLS = 128
+GPSIMD_COLS = 128
+SCALAR_COLS = 192
 SCALAR_COPIES = (N_TILE - GPSIMD_COLS) // SCALAR_COLS
 TOKENS_AHEAD = 2
 

@@ -91,12 +91,14 @@ def tile_reasoningmultiheadattention_pa_kernel(
 
         def load_weight(phase, g):
             stage, r = phase // 2, phase % 2
-            nc.sync.dma_start(
-                out=w_raw[:, phase, g, :, :],
-                in_=weights[stage // CHUNKS][r][
-                    g * K_PASS : (g + 1) * K_PASS, columns(stage)
-                ].rearrange("(p t) n -> p t n", t=PACK),
-            )
+            for u in range(2):
+                first = g * K_PASS + u * (K_PASS // 2)
+                nc.sync.dma_start(
+                    out=w_raw[:, phase, g, 2 * u : 2 * u + 2, :],
+                    in_=weights[stage // CHUNKS][r][
+                        first : first + K_PASS // 2, columns(stage)
+                    ].rearrange("(p e) n -> p e n", e=2),
+                )
 
         def load_tokens(m):
             nc.sync.dma_start(out=x_raw[:, m, :], in_=x_rows[m * P : (m + 1) * P, :])
@@ -123,7 +125,7 @@ def tile_reasoningmultiheadattention_pa_kernel(
             )
 
         def quantise_tokens(m):
-            words = x_raw[:, m, :].bitcast(F32).rearrange("r (g p u) -> r g u p", g=PASSES, u=2)
+            words = x_raw[:, m, :].bitcast(F32).rearrange("r (g u p) -> r g u p", g=PASSES, u=2)
             turned = side_banks.tile([P, PASSES, 2, P], F32, name="side")
             for g in range(PASSES):
                 for u in range(2):

@@ -30,11 +30,12 @@ RUN = 4
 GPSIMD_COLS = 128
 SCALAR_COLS = 192
 SCALAR_COPIES = (N_TILE - GPSIMD_COLS) // SCALAR_COLS
+BIAS_FIRST = 3
 TOKENS_AHEAD = 2
 
 FLOPS = 4 * 2 * TOKENS * HID * DQ
 
-ROW_ONE, ROW_GATE, ROW_MINUS_GATE = 0, 32, 64
+ROW_ONE, ROW_MINUS_GATE, ROW_GATE = 0, 32, 64
 
 
 def regroup(copy, grouped, rows):
@@ -49,7 +50,7 @@ def tile_reasoningmultiheadattention_pa_kernel(
 ):
     nc = tc.nc
     x_rows = x.flatten_outer_dims()
-    gate_row = reasoning_mask.rearrange("b s o i -> (o i) (b s)")
+    gate_flat = reasoning_mask.rearrange("b s o i -> (b s o i)")
     outs = (out_0.rearrange("b s h d -> (b s) (h d)"), out_1.rearrange("b s h d -> (b s) (h d)"))
     weights = ((Wq, Wqr), (Wk, Wkr))
     biases = ((bq, bqr), (bk, bkr))
@@ -84,10 +85,13 @@ def tile_reasoningmultiheadattention_pa_kernel(
 
         def load_bias_rows(o):
             plain, reasoning = biases[o]
-            for row, bias in ((ROW_ONE, plain), (ROW_GATE, reasoning), (ROW_MINUS_GATE, plain)):
-                nc.sync.dma_start(
-                    out=blend_rhs[o][row : row + 1, :], in_=bias.rearrange("(o n) -> o n", o=1)
-                )
+            nc.sync.dma_start(
+                out=blend_rhs[o][ROW_ONE : ROW_MINUS_GATE + 1 : ROW_MINUS_GATE - ROW_ONE, :],
+                in_=plain.partition_broadcast(2),
+            )
+            nc.sync.dma_start(
+                out=blend_rhs[o][ROW_GATE : ROW_GATE + 1, :], in_=reasoning.rearrange("(o n) -> o n", o=1)
+            )
 
         def load_weight(phase, g):
             stage, r = phase // 2, phase % 2
@@ -178,19 +182,22 @@ def tile_reasoningmultiheadattention_pa_kernel(
                     in_=acc[:, stage, m, :],
                 )
 
-        nc.vector.memset(blend_lhs[:].bitcast(I32), 0)
-        nc.vector.memset(blend_lhs[ROW_ONE : ROW_ONE + 32, :], 1.0)
+        nc.gpsimd.memset(blend_lhs[:].bitcast(F32), 0.0)
         nc.vector.memset(blend_rhs[0][:].bitcast(I32), 0)
+        nc.vector.memset(blend_lhs[ROW_ONE : ROW_ONE + 32, :], 1.0)
         nc.vector.memset(blend_rhs[1][:].bitcast(I32), 0)
         make_identity(nc, ident_f32[:])
         make_identity(nc, ident_bf16[:])
-        nc.sync.dma_start(out=blend_lhs[ROW_GATE : ROW_GATE + 1, :], in_=gate_row)
-        nc.sync.dma_start(out=blend_lhs[ROW_MINUS_GATE : ROW_MINUS_GATE + 1, :], in_=gate_row)
+        nc.sync.dma_start(
+            out=blend_lhs[ROW_MINUS_GATE : ROW_GATE + 1 : ROW_GATE - ROW_MINUS_GATE, :],
+            in_=gate_flat.partition_broadcast(2),
+        )
         load_bias_rows(0)
+        load_tokens(0)
         for g in range(PASSES):
             load_weight(0, g)
         for g in range(PASSES):
-            for m in range(g * STEPS_PER_PASS, (g + 1) * STEPS_PER_PASS):
+            for m in range(max(1, g * STEPS_PER_PASS), (g + 1) * STEPS_PER_PASS):
                 load_tokens(m)
             load_weight(1, g)
         load_bias_rows(1)
@@ -203,11 +210,15 @@ def tile_reasoningmultiheadattention_pa_kernel(
             scalar1=-1.0,
         )
 
-        for m in range(TOKEN_TILES):
+        for m in range(BIAS_FIRST):
             blended_bias(0, m)
-        for g in range(PASSES):
-            regroup_weight(nc.vector.tensor_copy, 0, g, 0, N_TILE)
-            quantise_weight(0, g)
+        regroup_weight(nc.vector.tensor_copy, 0, 0, 0, N_TILE)
+        quantise_tokens(0)
+        quantise_weight(0, 0)
+        regroup_weight(nc.vector.tensor_copy, 0, 1, 0, N_TILE)
+        for m in range(BIAS_FIRST, TOKEN_TILES):
+            blended_bias(0, m)
+        quantise_weight(0, 1)
         lhs_turned = side_banks.tile([P, TOKEN_TILES, P], BF16, name="side")
         for m in range(TOKEN_TILES):
             nc.tensor.transpose(lhs_turned[:, m, :], blend_lhs[:, m * P : (m + 1) * P], ident_bf16[:])
@@ -215,7 +226,7 @@ def tile_reasoningmultiheadattention_pa_kernel(
         nc.vector.tensor_scalar(
             out=one_minus_gate[:], in0=gate[:], scalar1=-1.0, scalar2=1.0, op0=MULT, op1=ADD
         )
-        for m in range(TOKENS_AHEAD):
+        for m in range(1, TOKENS_AHEAD):
             quantise_tokens(m)
 
         for phase in range(PHASES):

@@ -30,6 +30,7 @@ RUN = 4
 GPSIMD_COLS = 128
 SCALAR_COLS = 192
 SCALAR_COPIES = (N_TILE - GPSIMD_COLS) // SCALAR_COLS
+BIAS_STEP = 2
 BIAS_FIRST = 3
 TOKENS_AHEAD = 2
 
@@ -58,7 +59,7 @@ def tile_reasoningmultiheadattention_pa_kernel(
     with ExitStack() as stack:
         stack.enter_context(tc.manual_schedule())
         keep = stack.enter_context(tc.tile_pool(name="keep", bufs=1))
-        w_stage = stack.enter_context(tc.tile_pool(name="w_stage", bufs=3))
+        w_stage = stack.enter_context(tc.tile_pool(name="w_stage", bufs=2))
         x_stage = stack.enter_context(tc.tile_pool(name="x_stage", bufs=4))
         product_banks = stack.enter_context(tc.psum_pool(name="product_banks", bufs=4))
         side_banks = stack.enter_context(tc.psum_pool(name="side_banks", bufs=4))
@@ -77,6 +78,7 @@ def tile_reasoningmultiheadattention_pa_kernel(
         w_codes = keep.tile([P, PHASES, PASSES, N_TILE], U32, align_bytes=64)
         w_scales = keep.tile([P, PHASES, PASSES, N_TILE], U8, align_bytes=64)
         acc = keep.tile([P, STAGES, TOKEN_TILES, N_TILE], F32)
+        turned_of = {}
         grouped_of = {}
 
         def columns(stage):
@@ -129,11 +131,19 @@ def tile_reasoningmultiheadattention_pa_kernel(
             )
 
         def quantise_tokens(m):
+            transpose_tokens(m)
+            finish_tokens(m)
+
+        def transpose_tokens(m):
             words = x_raw[:, m, :].bitcast(F32).rearrange("r (g u p) -> r g u p", g=PASSES, u=2)
             turned = side_banks.tile([P, PASSES, 2, P], F32, name="side")
             for g in range(PASSES):
                 for u in range(2):
                     nc.tensor.transpose(turned[:, g, u, :], words[:, g, u, :], ident_f32[:])
+            turned_of[m] = turned
+
+        def finish_tokens(m):
+            turned = turned_of[m]
             x_grouped = x_stage.tile([P, PASSES * P * PACK], BF16, align_bytes=64)
             nc.scalar.copy(
                 out=x_grouped[:].bitcast(F32).rearrange("p (g r u) -> p g r u", g=PASSES, u=2),
@@ -234,7 +244,10 @@ def tile_reasoningmultiheadattention_pa_kernel(
             for m in range(TOKEN_TILES):
                 g, step = m // STEPS_PER_PASS, m % STEPS_PER_PASS
                 if phase == 0 and m + TOKENS_AHEAD < TOKEN_TILES:
-                    quantise_tokens(m + TOKENS_AHEAD)
+                    if m % 2 == 0:
+                        transpose_tokens(m + TOKENS_AHEAD)
+                        transpose_tokens(m + TOKENS_AHEAD + 1)
+                    finish_tokens(m + TOKENS_AHEAD)
                 if phase + 1 < PHASES:
                     if step == 0:
                         regroup_weight(gpsimd_copy, phase + 1, g, 0, GPSIMD_COLS)
@@ -242,8 +255,9 @@ def tile_reasoningmultiheadattention_pa_kernel(
                         regroup_weight(
                             nc.scalar.copy, phase + 1, g, GPSIMD_COLS + step * SCALAR_COLS, SCALAR_COLS
                         )
-                if stage + 1 < STAGES and m % 2 == 1:
-                    blended_bias(stage + 1, (r * TOKEN_TILES + m) // 2)
+                if stage + 1 < STAGES and step == BIAS_STEP:
+                    for tile in range(2):
+                        blended_bias(stage + 1, (r * TOKEN_TILES + m) // STEPS_PER_PASS * 2 + tile)
                 multiply_and_blend(phase, m)
                 if phase + 1 < PHASES and step == SCALAR_COPIES - 1:
                     quantise_weight(phase + 1, g)

@@ -31,7 +31,6 @@ GPSIMD_COLS = 128
 SCALAR_COLS = 192
 SCALAR_COPIES = (N_TILE - GPSIMD_COLS) // SCALAR_COLS
 BIAS_STEP = 2
-BIAS_FIRST = 3
 TOKENS_AHEAD = 2
 
 FLOPS = 4 * 2 * TOKENS * HID * DQ
@@ -162,7 +161,10 @@ def tile_reasoningmultiheadattention_pa_kernel(
                 start=True,
                 stop=True,
             )
-            nc.scalar.copy(out=acc[:, stage, m, :], in_=bias_bank[:])
+            if (stage, m) == (0, 0):
+                nc.vector.tensor_copy(out=acc[:, stage, m, :], in_=bias_bank[:])
+            else:
+                nc.scalar.copy(out=acc[:, stage, m, :], in_=bias_bank[:])
 
         def multiply_and_blend(phase, m):
             stage, r = phase // 2, phase % 2
@@ -198,12 +200,12 @@ def tile_reasoningmultiheadattention_pa_kernel(
         nc.vector.memset(blend_rhs[1][:].bitcast(I32), 0)
         make_identity(nc, ident_f32[:])
         make_identity(nc, ident_bf16[:])
+        load_tokens(0)
         nc.sync.dma_start(
             out=blend_lhs[ROW_MINUS_GATE : ROW_GATE + 1 : ROW_GATE - ROW_MINUS_GATE, :],
             in_=gate_flat.partition_broadcast(2),
         )
         load_bias_rows(0)
-        load_tokens(0)
         for g in range(PASSES):
             load_weight(0, g)
         for g in range(PASSES):
@@ -220,14 +222,12 @@ def tile_reasoningmultiheadattention_pa_kernel(
             scalar1=-1.0,
         )
 
-        for m in range(BIAS_FIRST):
+        quantise_tokens(0)
+        for m in range(TOKEN_TILES):
             blended_bias(0, m)
         regroup_weight(nc.vector.tensor_copy, 0, 0, 0, N_TILE)
-        quantise_tokens(0)
-        quantise_weight(0, 0)
         regroup_weight(nc.vector.tensor_copy, 0, 1, 0, N_TILE)
-        for m in range(BIAS_FIRST, TOKEN_TILES):
-            blended_bias(0, m)
+        quantise_weight(0, 0)
         quantise_weight(0, 1)
         lhs_turned = side_banks.tile([P, TOKEN_TILES, P], BF16, name="side")
         for m in range(TOKEN_TILES):

@@ -27,8 +27,9 @@ PHASES = 2 * STAGES
 STEPS_PER_PASS = TOKEN_TILES // PASSES
 
 RUN = 4
-GPSIMD_COLS = 128
-SCALAR_COLS = 192
+GPSIMD_COLS = 192
+GPSIMD_COPIES = 2
+SCALAR_COLS = 160
 SCALAR_COPIES = (N_TILE - GPSIMD_COLS) // SCALAR_COLS
 BIAS_STEP = 2
 TOKENS_AHEAD = 2
@@ -116,11 +117,12 @@ def tile_reasoningmultiheadattention_pa_kernel(
                 grouped_of[(phase, g)] = w_stage.tile(
                     [P, N_TILE, PACK], BF16, align_bytes=64, name="grouped"
                 )
-            regroup(
-                copy,
-                grouped_of[(phase, g)][:, first : first + count, :],
-                w_raw[:, phase, g, :, first : first + count],
-            )
+            grouped = grouped_of[(phase, g)][:, first : first + count, :]
+            rows = w_raw[:, phase, g, :, first : first + count]
+            if copy is gpsimd_copy:
+                copy(out=grouped, in_=rows.rearrange("p t n -> p n t"))
+            else:
+                regroup(copy, grouped, rows)
 
         def quantise_weight(phase, g):
             nc.vector.quantize_mx(
@@ -250,7 +252,9 @@ def tile_reasoningmultiheadattention_pa_kernel(
                     finish_tokens(m + TOKENS_AHEAD)
                 if phase + 1 < PHASES:
                     if step == 0:
-                        regroup_weight(gpsimd_copy, phase + 1, g, 0, GPSIMD_COLS)
+                        piece = GPSIMD_COLS // GPSIMD_COPIES
+                        for i in range(GPSIMD_COPIES):
+                            regroup_weight(gpsimd_copy, phase + 1, g, i * piece, piece)
                     if step < SCALAR_COPIES:
                         regroup_weight(
                             nc.scalar.copy, phase + 1, g, GPSIMD_COLS + step * SCALAR_COLS, SCALAR_COLS

@@ -11,6 +11,7 @@ I32 = mybir.dt.int32
 FP8X4 = mybir.dt.float8_e4m3fn_x4
 MULT = mybir.AluOpType.mult
 ADD = mybir.AluOpType.add
+COPY = mybir.ActivationFunctionType.Copy
 
 P = 128
 PACK = 4
@@ -33,6 +34,7 @@ SCALAR_COLS = 160
 SCALAR_COPIES = (N_TILE - GPSIMD_COLS) // SCALAR_COLS
 BIAS_STEP = 2
 TOKENS_AHEAD = 2
+HANDED_OVER = ((6, 4), (6, 6))
 
 FLOPS = 4 * 2 * TOKENS * HID * DQ
 
@@ -61,6 +63,7 @@ def tile_reasoningmultiheadattention_pa_kernel(
         keep = stack.enter_context(tc.tile_pool(name="keep", bufs=1))
         w_stage = stack.enter_context(tc.tile_pool(name="w_stage", bufs=2))
         x_stage = stack.enter_context(tc.tile_pool(name="x_stage", bufs=4))
+        scaled_stage = stack.enter_context(tc.tile_pool(name="scaled_stage", bufs=2))
         product_banks = stack.enter_context(tc.psum_pool(name="product_banks", bufs=4))
         side_banks = stack.enter_context(tc.psum_pool(name="side_banks", bufs=4))
 
@@ -182,14 +185,15 @@ def tile_reasoningmultiheadattention_pa_kernel(
                     start=(g == 0),
                     stop=(g == PASSES - 1),
                 )
-            nc.vector.scalar_tensor_tensor(
-                out=acc[:, stage, m, :],
-                in0=product[:],
-                scalar=factor[r][:, m : m + 1],
-                in1=acc[:, stage, m, :],
-                op0=MULT,
-                op1=ADD,
-            )
+            blended = acc[:, stage, m, :]
+            if (phase, m) in HANDED_OVER:
+                scaled = scaled_stage.tile([P, N_TILE], F32)
+                nc.scalar.activation(out=scaled[:], in_=product[:], func=COPY, scale=factor[r][:, m : m + 1])
+                nc.gpsimd.tensor_tensor(out=blended, in0=blended, in1=scaled[:], op=ADD)
+            else:
+                nc.vector.scalar_tensor_tensor(
+                    out=blended, in0=product[:], scalar=factor[r][:, m : m + 1], in1=blended, op0=MULT, op1=ADD
+                )
             if r == 1:
                 nc.sync.dma_start(
                     out=outs[stage // CHUNKS][m * P : (m + 1) * P, columns(stage)],
@@ -251,17 +255,22 @@ def tile_reasoningmultiheadattention_pa_kernel(
                         transpose_tokens(m + TOKENS_AHEAD + 1)
                     finish_tokens(m + TOKENS_AHEAD)
                 if phase + 1 < PHASES:
-                    if step == 0:
-                        piece = GPSIMD_COLS // GPSIMD_COPIES
-                        for i in range(GPSIMD_COPIES):
-                            regroup_weight(gpsimd_copy, phase + 1, g, i * piece, piece)
-                    if step < SCALAR_COPIES:
-                        regroup_weight(
-                            nc.scalar.copy, phase + 1, g, GPSIMD_COLS + step * SCALAR_COLS, SCALAR_COLS
-                        )
+                    for g in range(PASSES):
+                        first = 3 if (phase + 2 == PHASES and g == 1) else g * STEPS_PER_PASS
+                        if m == first:
+                            piece = GPSIMD_COLS // GPSIMD_COPIES
+                            for i in range(GPSIMD_COPIES):
+                                regroup_weight(gpsimd_copy, phase + 1, g, i * piece, piece)
+                        if 0 <= m - first < SCALAR_COPIES:
+                            regroup_weight(
+                                nc.scalar.copy, phase + 1, g, GPSIMD_COLS + (m - first) * SCALAR_COLS, SCALAR_COLS
+                            )
                 if stage + 1 < STAGES and step == BIAS_STEP:
                     for tile in range(2):
                         blended_bias(stage + 1, (r * TOKEN_TILES + m) // STEPS_PER_PASS * 2 + tile)
                 multiply_and_blend(phase, m)
-                if phase + 1 < PHASES and step == SCALAR_COPIES - 1:
-                    quantise_weight(phase + 1, g)
+                if phase + 1 < PHASES:
+                    for g in range(PASSES):
+                        due = ((1, 4))[g] if phase + 2 == PHASES else g * STEPS_PER_PASS + 1
+                        if m == due:
+                            quantise_weight(phase + 1, g)

from contextlib import ExitStack

import concourse.mybir as mybir
from concourse.masks import make_identity

F32 = mybir.dt.float32
BF16 = mybir.dt.bfloat16
U32 = mybir.dt.uint32
U8 = mybir.dt.uint8
I32 = mybir.dt.int32
FP8X4 = mybir.dt.float8_e4m3fn_x4
MULT = mybir.AluOpType.mult
ADD = mybir.AluOpType.add
COPY = mybir.ActivationFunctionType.Copy

P = 128
PACK = 4
K_PASS = P * PACK
TOKENS = 1024
HID = 1024
DQ = 1024
PASSES = HID // K_PASS
TOKEN_TILES = TOKENS // P
N_TILE = 512
CHUNKS = DQ // N_TILE
STAGES = 2 * CHUNKS
PHASES = 2 * STAGES
STEPS_PER_PASS = TOKEN_TILES // PASSES

RUN = 4
GPSIMD_COLS = 192
GPSIMD_COPIES = 2
SCALAR_COLS = 160
SCALAR_COPIES = (N_TILE - GPSIMD_COLS) // SCALAR_COLS
BIAS_STEP = 2
TOKENS_AHEAD = 2
HANDED_OVER = ((6, 4), (6, 6))

FLOPS = 4 * 2 * TOKENS * HID * DQ

ROW_ONE, ROW_MINUS_GATE, ROW_GATE = 0, 32, 64


def regroup(copy, grouped, rows):
    copy(
        out=grouped.rearrange("p (c i) t -> p c t i", i=RUN),
        in_=rows.rearrange("p t (c i) -> p c t i", i=RUN),
    )


def tile_reasoningmultiheadattention_pa_kernel(
    tc, x, reasoning_mask, Wq, bq, Wk, bk, Wqr, bqr, Wkr, bkr, out_0, out_1
):
    nc = tc.nc
    x_rows = x.flatten_outer_dims()
    gate_flat = reasoning_mask.rearrange("b s o i -> (b s o i)")
    outs = (out_0.rearrange("b s h d -> (b s) (h d)"), out_1.rearrange("b s h d -> (b s) (h d)"))
    weights = ((Wq, Wqr), (Wk, Wkr))
    biases = ((bq, bqr), (bk, bkr))

    with ExitStack() as stack:
        stack.enter_context(tc.manual_schedule())
        keep = stack.enter_context(tc.tile_pool(name="keep", bufs=1))
        w_stage = stack.enter_context(tc.tile_pool(name="w_stage", bufs=2))
        x_stage = stack.enter_context(tc.tile_pool(name="x_stage", bufs=4))
        scaled_stage = stack.enter_context(tc.tile_pool(name="scaled_stage", bufs=2))
        product_banks = stack.enter_context(tc.psum_pool(name="product_banks", bufs=4))
        side_banks = stack.enter_context(tc.psum_pool(name="side_banks", bufs=4))

        blend_lhs = keep.tile([P, TOKENS], BF16)
        blend_rhs = [keep.tile([P, DQ], BF16, name="blend_rhs_%d" % o) for o in range(2)]
        ident_f32 = keep.tile([P, P], F32)
        ident_bf16 = keep.tile([P, P], BF16)
        gate = keep.tile([P, TOKEN_TILES], F32)
        one_minus_gate = keep.tile([P, TOKEN_TILES], F32)
        factor = (one_minus_gate, gate)
        x_raw = keep.tile([P, TOKEN_TILES, HID], BF16)
        w_raw = keep.tile([P, PHASES, PASSES, PACK, N_TILE], BF16)
        x_codes = keep.tile([P, TOKEN_TILES, PASSES * P], U32, align_bytes=64)
        x_scales = keep.tile([P, TOKEN_TILES, PASSES * P], U8, align_bytes=64)
        w_codes = keep.tile([P, PHASES, PASSES, N_TILE], U32, align_bytes=64)
        w_scales = keep.tile([P, PHASES, PASSES, N_TILE], U8, align_bytes=64)
        acc = keep.tile([P, STAGES, TOKEN_TILES, N_TILE], F32)
        turned_of = {}
        grouped_of = {}

        def columns(stage):
            chunk = stage % CHUNKS
            return slice(chunk * N_TILE, (chunk + 1) * N_TILE)

        def load_bias_rows(o):
            plain, reasoning = biases[o]
            nc.sync.dma_start(
                out=blend_rhs[o][ROW_ONE : ROW_MINUS_GATE + 1 : ROW_MINUS_GATE - ROW_ONE, :],
                in_=plain.partition_broadcast(2),
            )
            nc.sync.dma_start(
                out=blend_rhs[o][ROW_GATE : ROW_GATE + 1, :], in_=reasoning.rearrange("(o n) -> o n", o=1)
            )

        def load_weight(phase, g):
            stage, r = phase // 2, phase % 2
            for u in range(2):
                first = g * K_PASS + u * (K_PASS // 2)
                nc.sync.dma_start(
                    out=w_raw[:, phase, g, 2 * u : 2 * u + 2, :],
                    in_=weights[stage // CHUNKS][r][
                        first : first + K_PASS // 2, columns(stage)
                    ].rearrange("(p e) n -> p e n", e=2),
                )

        def load_tokens(m):
            nc.sync.dma_start(out=x_raw[:, m, :], in_=x_rows[m * P : (m + 1) * P, :])

        def gpsimd_copy(out, in_):
            nc.gpsimd.tensor_scalar(out=out, in0=in_, scalar1=1.0, scalar2=0.0, op0=MULT, op1=ADD)

        def regroup_weight(copy, phase, g, first, count):
            if (phase, g) not in grouped_of:
                grouped_of[(phase, g)] = w_stage.tile(
                    [P, N_TILE, PACK], BF16, align_bytes=64, name="grouped"
                )
            grouped = grouped_of[(phase, g)][:, first : first + count, :]
            rows = w_raw[:, phase, g, :, first : first + count]
            if copy is gpsimd_copy:
                copy(out=grouped, in_=rows.rearrange("p t n -> p n t"))
            else:
                regroup(copy, grouped, rows)

        def quantise_weight(phase, g):
            nc.vector.quantize_mx(
                out=w_codes[:, phase, g, :].bitcast(FP8X4),
                scales=w_scales[:, phase, g, :],
                in_=grouped_of[(phase, g)][:].rearrange("p n t -> p (n t)"),
            )

        def quantise_tokens(m):
            transpose_tokens(m)
            finish_tokens(m)

        def transpose_tokens(m):
            words = x_raw[:, m, :].bitcast(F32).rearrange("r (g u p) -> r g u p", g=PASSES, u=2)
            turned = side_banks.tile([P, PASSES, 2, P], F32, name="side")
            for g in range(PASSES):
                for u in range(2):
                    nc.tensor.transpose(turned[:, g, u, :], words[:, g, u, :], ident_f32[:])
            turned_of[m] = turned

        def finish_tokens(m):
            turned = turned_of[m]
            x_grouped = x_stage.tile([P, PASSES * P * PACK], BF16, align_bytes=64)
            nc.scalar.copy(
                out=x_grouped[:].bitcast(F32).rearrange("p (g r u) -> p g r u", g=PASSES, u=2),
                in_=turned[:].rearrange("p g u r -> p g r u"),
            )
            nc.vector.quantize_mx(
                out=x_codes[:, m, :].bitcast(FP8X4), scales=x_scales[:, m, :], in_=x_grouped[:]
            )

        def blended_bias(stage, m):
            bias_bank = side_banks.tile([P, N_TILE], F32, name="side")
            nc.tensor.matmul(
                out=bias_bank[:],
                lhsT=blend_lhs[:, m * P : (m + 1) * P],
                rhs=blend_rhs[stage // CHUNKS][:, columns(stage)],
                start=True,
                stop=True,
            )
            if (stage, m) == (0, 0):
                nc.vector.tensor_copy(out=acc[:, stage, m, :], in_=bias_bank[:])
            else:
                nc.scalar.copy(out=acc[:, stage, m, :], in_=bias_bank[:])

        def multiply_and_blend(phase, m):
            stage, r = phase // 2, phase % 2
            product = product_banks.tile([P, N_TILE], F32)
            for g in range(PASSES):
                tokens = slice(g * P, (g + 1) * P)
                nc.tensor.matmul_mx(
                    out=product[:],
                    lhsT=x_codes[:, m, tokens].bitcast(FP8X4),
                    lhsT_scale=x_scales[:, m, tokens],
                    rhs=w_codes[:, phase, g, :].bitcast(FP8X4),
                    rhs_scale=w_scales[:, phase, g, :],
                    start=(g == 0),
                    stop=(g == PASSES - 1),
                )
            blended = acc[:, stage, m, :]
            if (phase, m) in HANDED_OVER:
                scaled = scaled_stage.tile([P, N_TILE], F32)
                nc.scalar.activation(out=scaled[:], in_=product[:], func=COPY, scale=factor[r][:, m : m + 1])
                nc.gpsimd.tensor_tensor(out=blended, in0=blended, in1=scaled[:], op=ADD)
            else:
                nc.vector.scalar_tensor_tensor(
                    out=blended, in0=product[:], scalar=factor[r][:, m : m + 1], in1=blended, op0=MULT, op1=ADD
                )
            if r == 1:
                nc.sync.dma_start(
                    out=outs[stage // CHUNKS][m * P : (m + 1) * P, columns(stage)],
                    in_=acc[:, stage, m, :],
                )

        nc.gpsimd.memset(blend_lhs[:].bitcast(F32), 0.0)
        nc.vector.memset(blend_rhs[0][:].bitcast(I32), 0)
        nc.vector.memset(blend_lhs[ROW_ONE : ROW_ONE + 32, :], 1.0)
        nc.vector.memset(blend_rhs[1][:].bitcast(I32), 0)
        make_identity(nc, ident_f32[:])
        make_identity(nc, ident_bf16[:])
        load_tokens(0)
        nc.sync.dma_start(
            out=blend_lhs[ROW_MINUS_GATE : ROW_GATE + 1 : ROW_GATE - ROW_MINUS_GATE, :],
            in_=gate_flat.partition_broadcast(2),
        )
        load_bias_rows(0)
        for g in range(PASSES):
            load_weight(0, g)
        for g in range(PASSES):
            for m in range(max(1, g * STEPS_PER_PASS), (g + 1) * STEPS_PER_PASS):
                load_tokens(m)
            load_weight(1, g)
        load_bias_rows(1)
        for phase in range(2, PHASES):
            for g in range(PASSES):
                load_weight(phase, g)
        nc.vector.tensor_scalar_mul(
            out=blend_lhs[ROW_MINUS_GATE : ROW_MINUS_GATE + 32, :],
            in0=blend_lhs[ROW_MINUS_GATE : ROW_MINUS_GATE + 32, :],
            scalar1=-1.0,
        )

        quantise_tokens(0)
        for m in range(TOKEN_TILES):
            blended_bias(0, m)
        regroup_weight(nc.vector.tensor_copy, 0, 0, 0, N_TILE)
        regroup_weight(nc.vector.tensor_copy, 0, 1, 0, N_TILE)
        quantise_weight(0, 0)
        quantise_weight(0, 1)
        lhs_turned = side_banks.tile([P, TOKEN_TILES, P], BF16, name="side")
        for m in range(TOKEN_TILES):
            nc.tensor.transpose(lhs_turned[:, m, :], blend_lhs[:, m * P : (m + 1) * P], ident_bf16[:])
        nc.vector.tensor_copy(out=gate[:], in_=lhs_turned[:, :, ROW_GATE])
        nc.vector.tensor_scalar(
            out=one_minus_gate[:], in0=gate[:], scalar1=-1.0, scalar2=1.0, op0=MULT, op1=ADD
        )
        for m in range(1, TOKENS_AHEAD):
            quantise_tokens(m)

        for phase in range(PHASES):
            stage, r = phase // 2, phase % 2
            for m in range(TOKEN_TILES):
                g, step = m // STEPS_PER_PASS, m % STEPS_PER_PASS
                if phase == 0 and m + TOKENS_AHEAD < TOKEN_TILES:
                    if m % 2 == 0:
                        transpose_tokens(m + TOKENS_AHEAD)
                        transpose_tokens(m + TOKENS_AHEAD + 1)
                    finish_tokens(m + TOKENS_AHEAD)
                if phase + 1 < PHASES:
                    for g in range(PASSES):
                        first = 3 if (phase + 2 == PHASES and g == 1) else g * STEPS_PER_PASS
                        if m == first:
                            piece = GPSIMD_COLS // GPSIMD_COPIES
                            for i in range(GPSIMD_COPIES):
                                regroup_weight(gpsimd_copy, phase + 1, g, i * piece, piece)
                        if 0 <= m - first < SCALAR_COPIES:
                            regroup_weight(
                                nc.scalar.copy, phase + 1, g, GPSIMD_COLS + (m - first) * SCALAR_COLS, SCALAR_COLS
                            )
                if stage + 1 < STAGES and step == BIAS_STEP:
                    for tile in range(2):
                        blended_bias(stage + 1, (r * TOKEN_TILES + m) // STEPS_PER_PASS * 2 + tile)
                multiply_and_blend(phase, m)
                if phase + 1 < PHASES:
                    for g in range(PASSES):
                        due = ((1, 4))[g] if phase + 2 == PHASES else g * STEPS_PER_PASS + 1
                        if m == due:
                            quantise_weight(phase + 1, g)
